import numpy as np
import ml_dtypes


def mxq(x, axis, fmt="e4m3"):
    dtype, down = {"e4m3": (ml_dtypes.float8_e4m3fn, 7), "e5m2": (ml_dtypes.float8_e5m2, 14)}[fmt]
    v = np.moveaxis(np.asarray(x, np.float32).astype(ml_dtypes.bfloat16).astype(np.float64), axis, -1)
    blocks = v.reshape(v.shape[:-1] + (-1, 32))
    amax = np.abs(blocks).max(-1, keepdims=True)
    byte = np.maximum(np.where(amax > 0, np.frexp(amax)[1] - 1 + 127, 0) - down, 1)
    scale = np.exp2(byte - 127.0)
    codes = (blocks / scale).astype(np.float32).astype(dtype).astype(np.float64)
    return np.moveaxis((codes * scale).reshape(v.shape), -1, axis)


WIDE = False


def mx_kscale(k):
    if not WIDE:
        return np.ones(k)
    levels = np.array([10, -10, 5, -5, 0])
    a = np.random.permutation(np.resize(levels, k // 512 * 4)).reshape(k // 512, 4)
    idx = np.arange(k)
    return np.exp2(a[idx // 512, idx % 128 // 32])


BF16 = ml_dtypes.bfloat16


def bf(x):
    return np.asarray(x, np.float32).astype(BF16)


def f64(x):
    return np.asarray(x).astype(np.float64)


B, C, N = 2, 16, 512
NH = N // 2


def setup_inputs():
    u = np.where(np.arange(N) < NH, 1.0, mx_kscale(N))
    return {"x": bf(np.random.standard_normal((B, C, N, N)) * u),
            "haar": bf(np.random.standard_normal((N, N)) / np.sqrt(N) * u[None, :] / u[:, None])}


def reference(x, haar):
    r = f64(x).transpose(0, 2, 1, 3).reshape(B, C, N, N)[:, :, :NH, :]
    hq = mxq(f64(haar), 0, "e4m3")
    t = mxq(r, 3, "e4m3") @ hq
    return mxq(t, 3, "e4m3") @ hq[:, :NH]

@@ -1,0 +1,172 @@
+from contextlib import ExitStack
+
+import concourse.mybir as mybir
+from concourse.masks import make_identity
+
+F32 = mybir.dt.float32
+BF16 = mybir.dt.bfloat16
+U32 = mybir.dt.uint32
+U8 = mybir.dt.uint8
+FP8X4 = mybir.dt.float8_e4m3fn_x4
+
+P = 128
+N = 512
+NH = 256
+ROWS = 8192
+FLOPS = 2 * ROWS * N * N + 2 * ROWS * N * NH
+BYTES = ROWS * N * 2 + N * N * 2 + ROWS * NH * 4
+NQ = 16
+
+
+def tile_mylayer_t_kernel(tc, x, haar, out):
+    nc = tc.nc
+    with ExitStack() as ctx:
+        const = ctx.enter_context(tc.tile_pool(name="const", bufs=1))
+        xpool = ctx.enter_context(tc.tile_pool(name="xpool", bufs=NQ))
+        work = ctx.enter_context(tc.tile_pool(name="work", bufs=2))
+        opool = ctx.enter_context(tc.tile_pool(name="opool", bufs=6))
+        ps_t = ctx.enter_context(tc.psum_pool(name="ps_t", bufs=2))
+        ps_1 = ctx.enter_context(tc.psum_pool(name="ps_1", bufs=4))
+        ps_2 = ctx.enter_context(tc.psum_pool(name="ps_2", bufs=2))
+        ctx.enter_context(tc.manual_schedule())
+
+        def x_view(q):
+            b, sg = (q // 4) // 2, (q // 4) % 2
+            v = x[b].rearrange("c (l s r) k -> s (c l) r k", l=8, s=2, r=32)
+            return v[sg][:, 4 * (q % 4) : 4 * (q % 4) + 4, :]
+
+        def out_view(q, s):
+            b, sg = (q // 4) // 2, (q // 4) % 2
+            v = out[b].rearrange("(l s) (i c) n -> s i c l n", s=2, c=16)
+            return v[sg][4 * (q % 4) + s]
+
+        ident = const.tile([P, P], F32, name="ident")
+        make_identity(nc, ident[:])
+
+        xq = {}
+        hraw = const.tile([P, 4, N], BF16, name="hraw")
+        for q in range(NQ):
+            xq[q] = xpool.tile([P, 4, N], BF16, name="xq", tag="xq")
+            if q == 0:
+                nc.sync.dma_start(out=xq[0][:, 0:2, :], in_=x_view(0)[:, 0:2, :])
+                nc.sync.dma_start(out=hraw[:], in_=haar.rearrange("(p j) w -> p j w", j=4))
+                nc.sync.dma_start(out=xq[0][:, 2:4, :], in_=x_view(0)[:, 2:4, :])
+            else:
+                nc.sync.dma_start(out=xq[q][:], in_=x_view(q))
+
+        g1 = const.tile([P, 4, P, 4], BF16, name="g1", align_bytes=64)
+        g2 = const.tile([P, NH, 4], BF16, name="g2", align_bytes=64)
+        h1c = const.tile([P, N], U32, name="h1c", align_bytes=64)
+        h1s = const.tile([P, N], U8, name="h1s", align_bytes=64)
+        h2c = const.tile([P, NH], U32, name="h2c", align_bytes=64)
+        h2s = const.tile([P, NH], U8, name="h2s", align_bytes=64)
+
+        tb, rg, rc, rs, s1b, tg, tq, ts, s2b, ob = {}, {}, {}, {}, {}, {}, {}, {}, {}, {}
+
+        def st_a(q):
+            xw = xq[q][:].bitcast(F32)
+            for h in range(2):
+                tb[q, h] = ps_t.tile([P, 2, 256], F32, name="tb", tag="tb")
+                for e in range(2):
+                    for u in range(2):
+                        nc.tensor.transpose(
+                            tb[q, h][:, u, e * P : (e + 1) * P], xw[:, 2 * h + e, u:256:2], ident[:]
+                        )
+
+        def st_b(q):
+            rg[q] = work.tile([P, 4 * N], BF16, name="rg", tag="rg", align_bytes=64)
+            rw = rg[q][:].bitcast(F32).rearrange("p (r u) -> p r u", u=2)
+            for h in range(2):
+                nc.vector.tensor_copy(
+                    out=rw[:, h * 256 : (h + 1) * 256, :], in_=tb[q, h][:].rearrange("p u r -> p r u")
+                )
+
+        def st_c(q):
+            rc[q] = work.tile([P, N], U32, name="rc", tag="rc", align_bytes=64)
+            rs[q] = work.tile([P, N], U8, name="rs", tag="rs", align_bytes=64)
+            for h in range(2):
+                nc.vector.quantize_mx(
+                    out=rc[q][:, h * 256 : (h + 1) * 256].bitcast(FP8X4),
+                    scales=rs[q][:, h * 256 : (h + 1) * 256],
+                    in_=rg[q][:, h * 1024 : (h + 1) * 1024],
+                )
+
+        def st_d(q):
+            for rt in range(4):
+                s1b[q, rt] = ps_1.tile([P, 4, P], F32, name="s1b", tag="s1b")
+                for a in range(4):
+                    nc.tensor.matmul_mx(
+                        out=s1b[q, rt][:, a, :],
+                        lhsT=h1c[:, a * P : (a + 1) * P].bitcast(FP8X4),
+                        lhsT_scale=h1s[:, a * P : (a + 1) * P],
+                        rhs=rc[q][:, rt * P : (rt + 1) * P].bitcast(FP8X4),
+                        rhs_scale=rs[q][:, rt * P : (rt + 1) * P],
+                        start=True,
+                        stop=True,
+                    )
+
+        def st_e(q):
+            tg[q] = work.tile([P, 4 * N], BF16, name="tg", tag="tg", align_bytes=64)
+            for rt in range(4):
+                nc.scalar.copy(
+                    out=tg[q][:, rt * N : (rt + 1) * N].rearrange("p (r a) -> p r a", a=4),
+                    in_=s1b[q, rt][:].rearrange("p a r -> p r a"),
+                )
+
+        def st_f(q):
+            tq[q] = work.tile([P, N], U32, name="tq", tag="tq", align_bytes=64)
+            ts[q] = work.tile([P, N], U8, name="ts", tag="ts", align_bytes=64)
+            nc.vector.quantize_mx(out=tq[q][:].bitcast(FP8X4), scales=ts[q][:], in_=tg[q][:])
+
+        def st_g(q):
+            for h in range(2):
+                s2b[q, h] = ps_2.tile([P, 2, NH], F32, name="s2b", tag="s2b")
+                for e in range(2):
+                    rt = 2 * h + e
+                    nc.tensor.matmul_mx(
+                        out=s2b[q, h][:, e, :],
+                        lhsT=tq[q][:, rt * P : (rt + 1) * P].bitcast(FP8X4),
+                        lhsT_scale=ts[q][:, rt * P : (rt + 1) * P],
+                        rhs=h2c[:].bitcast(FP8X4),
+                        rhs_scale=h2s[:],
+                        start=True,
+                        stop=True,
+                    )
+
+        def st_h(q):
+            ob[q] = opool.tile([P, 4, NH], F32, name="ob", tag="ob")
+            nc.vector.tensor_copy(out=ob[q][:, 0:2, :], in_=s2b[q, 0][:])
+            nc.scalar.copy(out=ob[q][:, 2:4, :], in_=s2b[q, 1][:])
+
+        def st_i(q):
+            for s in range(4):
+                nc.sync.dma_start(out=out_view(q, s), in_=ob[q][:, s, :])
+
+        st_a(0)
+        st_b(0)
+        nc.scalar.copy(out=g2[:], in_=hraw[:, :, 0:NH].rearrange("p j w -> p w j"))
+        nc.vector.tensor_copy(out=g1[:], in_=hraw[:].rearrange("p j (m a) -> p a m j", a=4))
+        st_c(0)
+        nc.vector.quantize_mx(
+            out=h1c[:].bitcast(FP8X4), scales=h1s[:], in_=g1[:].rearrange("p a m j -> p (a m j)")
+        )
+        nc.vector.quantize_mx(
+            out=h2c[:].bitcast(FP8X4), scales=h2s[:], in_=g2[:].rearrange("p w j -> p (w j)")
+        )
+
+        for i in range(NQ + 1):
+            if i + 1 < NQ:
+                st_a(i + 1)
+            if i >= 1:
+                st_f(i - 1)
+            if i + 1 < NQ:
+                st_b(i + 1)
+            if i < NQ:
+                st_d(i)
+                st_e(i)
+            if i + 1 < NQ:
+                st_c(i + 1)
+            if i >= 1:
+                st_g(i - 1)
+                st_h(i - 1)
+                st_i(i - 1)

@@ -16,6 +16,8 @@ ROWS = 8192
 FLOPS = 2 * ROWS * N * N + 2 * ROWS * N * NH
 BYTES = ROWS * N * 2 + N * N * 2 + ROWS * NH * 4
 NQ = 16
+V = "vector"
+A = "scalar"
 
 
 def tile_mylayer_t_kernel(tc, x, haar, out):
@@ -23,11 +25,9 @@ def tile_mylayer_t_kernel(tc, x, haar, out):
     with ExitStack() as ctx:
         const = ctx.enter_context(tc.tile_pool(name="const", bufs=1))
         xpool = ctx.enter_context(tc.tile_pool(name="xpool", bufs=NQ))
-        work = ctx.enter_context(tc.tile_pool(name="work", bufs=2))
+        work = ctx.enter_context(tc.tile_pool(name="work", bufs=4))
         opool = ctx.enter_context(tc.tile_pool(name="opool", bufs=6))
-        ps_t = ctx.enter_context(tc.psum_pool(name="ps_t", bufs=2))
-        ps_1 = ctx.enter_context(tc.psum_pool(name="ps_1", bufs=4))
-        ps_2 = ctx.enter_context(tc.psum_pool(name="ps_2", bufs=2))
+        psum = ctx.enter_context(tc.psum_pool(name="psum", bufs=1))
         ctx.enter_context(tc.manual_schedule())
 
         def x_view(q):
@@ -40,6 +40,12 @@ def tile_mylayer_t_kernel(tc, x, haar, out):
             v = out[b].rearrange("(l s) (i c) n -> s i c l n", s=2, c=16)
             return v[sg][4 * (q % 4) + s]
 
+        def copy_on(eng, dst, src):
+            if eng == V:
+                nc.vector.tensor_copy(out=dst, in_=src)
+            else:
+                nc.scalar.copy(out=dst, in_=src)
+
         ident = const.tile([P, P], F32, name="ident")
         make_identity(nc, ident[:])
 
@@ -49,10 +55,11 @@ def tile_mylayer_t_kernel(tc, x, haar, out):
             xq[q] = xpool.tile([P, 4, N], BF16, name="xq", tag="xq")
             if q == 0:
                 nc.sync.dma_start(out=xq[0][:, 0:2, :], in_=x_view(0)[:, 0:2, :])
-                nc.sync.dma_start(out=hraw[:], in_=haar.rearrange("(p j) w -> p j w", j=4))
                 nc.sync.dma_start(out=xq[0][:, 2:4, :], in_=x_view(0)[:, 2:4, :])
             else:
                 nc.sync.dma_start(out=xq[q][:], in_=x_view(q))
+            if q == 1:
+                nc.sync.dma_start(out=hraw[:], in_=haar.rearrange("(p j) w -> p j w", j=4))
 
         g1 = const.tile([P, 4, P, 4], BF16, name="g1", align_bytes=64)
         g2 = const.tile([P, NH, 4], BF16, name="g2", align_bytes=64)
@@ -61,112 +68,147 @@ def tile_mylayer_t_kernel(tc, x, haar, out):
         h2c = const.tile([P, NH], U32, name="h2c", align_bytes=64)
         h2s = const.tile([P, NH], U8, name="h2s", align_bytes=64)
 
-        tb, rg, rc, rs, s1b, tg, tq, ts, s2b, ob = {}, {}, {}, {}, {}, {}, {}, {}, {}, {}
+        ring = [0]
+        bank, rg, rc, rs, tg, tq, ts, ob = {}, {}, {}, {}, {}, {}, {}, {}
 
-        def st_a(q):
+        def new_bank(key):
+            k = ring[0] % 8
+            ring[0] = ring[0] + 1
+            bank[key] = psum.tile([P, N], F32, name="bank%d" % k, tag="bank%d" % k)
+            return bank[key]
+
+        def p_t(q, h):
             xw = xq[q][:].bitcast(F32)
-            for h in range(2):
-                tb[q, h] = ps_t.tile([P, 2, 256], F32, name="tb", tag="tb")
-                for e in range(2):
-                    for u in range(2):
-                        nc.tensor.transpose(
-                            tb[q, h][:, u, e * P : (e + 1) * P], xw[:, 2 * h + e, u:256:2], ident[:]
-                        )
+            b = new_bank(("T", q, h))[:].rearrange("p (u r) -> p u r", u=2)
+            for e in range(2):
+                for u in range(2):
+                    nc.tensor.transpose(b[:, u, e * P : (e + 1) * P], xw[:, 2 * h + e, u:256:2], ident[:])
 
-        def st_b(q):
-            rg[q] = work.tile([P, 4 * N], BF16, name="rg", tag="rg", align_bytes=64)
+        def e_t(q, h, eng):
+            if q not in rg:
+                rg[q] = work.tile([P, 4 * N], BF16, name="rg", tag="rg", align_bytes=64)
             rw = rg[q][:].bitcast(F32).rearrange("p (r u) -> p r u", u=2)
-            for h in range(2):
-                nc.vector.tensor_copy(
-                    out=rw[:, h * 256 : (h + 1) * 256, :], in_=tb[q, h][:].rearrange("p u r -> p r u")
-                )
+            copy_on(eng, rw[:, h * 256 : (h + 1) * 256, :], bank["T", q, h][:].rearrange("p (u r) -> p r u", u=2))
 
-        def st_c(q):
+        def c_q(q):
             rc[q] = work.tile([P, N], U32, name="rc", tag="rc", align_bytes=64)
             rs[q] = work.tile([P, N], U8, name="rs", tag="rs", align_bytes=64)
-            for h in range(2):
-                nc.vector.quantize_mx(
-                    out=rc[q][:, h * 256 : (h + 1) * 256].bitcast(FP8X4),
-                    scales=rs[q][:, h * 256 : (h + 1) * 256],
-                    in_=rg[q][:, h * 1024 : (h + 1) * 1024],
+            nc.vector.quantize_mx(out=rc[q][:].bitcast(FP8X4), scales=rs[q][:], in_=rg[q][:])
+
+        def p_s(q, rt):
+            b = new_bank(("S", q, rt))
+            for a in range(4):
+                nc.tensor.matmul_mx(
+                    out=b[:, a * P : (a + 1) * P],
+                    lhsT=h1c[:, a * P : (a + 1) * P].bitcast(FP8X4),
+                    lhsT_scale=h1s[:, a * P : (a + 1) * P],
+                    rhs=rc[q][:, rt * P : (rt + 1) * P].bitcast(FP8X4),
+                    rhs_scale=rs[q][:, rt * P : (rt + 1) * P],
+                    start=True,
+                    stop=True,
                 )
 
-        def st_d(q):
-            for rt in range(4):
-                s1b[q, rt] = ps_1.tile([P, 4, P], F32, name="s1b", tag="s1b")
-                for a in range(4):
-                    nc.tensor.matmul_mx(
-                        out=s1b[q, rt][:, a, :],
-                        lhsT=h1c[:, a * P : (a + 1) * P].bitcast(FP8X4),
-                        lhsT_scale=h1s[:, a * P : (a + 1) * P],
-                        rhs=rc[q][:, rt * P : (rt + 1) * P].bitcast(FP8X4),
-                        rhs_scale=rs[q][:, rt * P : (rt + 1) * P],
-                        start=True,
-                        stop=True,
-                    )
+        def e_s(q, rt, eng):
+            if q not in tg:
+                tg[q] = work.tile([P, 4 * N], BF16, name="tg", tag="tg", align_bytes=64)
+            copy_on(
+                eng,
+                tg[q][:, rt * N : (rt + 1) * N].rearrange("p (r a) -> p r a", a=4),
+                bank["S", q, rt][:].rearrange("p (a r) -> p r a", a=4),
+            )
 
-        def st_e(q):
-            tg[q] = work.tile([P, 4 * N], BF16, name="tg", tag="tg", align_bytes=64)
-            for rt in range(4):
-                nc.scalar.copy(
-                    out=tg[q][:, rt * N : (rt + 1) * N].rearrange("p (r a) -> p r a", a=4),
-                    in_=s1b[q, rt][:].rearrange("p a r -> p r a"),
-                )
-
-        def st_f(q):
+        def f_q(q, parts):
             tq[q] = work.tile([P, N], U32, name="tq", tag="tq", align_bytes=64)
             ts[q] = work.tile([P, N], U8, name="ts", tag="ts", align_bytes=64)
-            nc.vector.quantize_mx(out=tq[q][:].bitcast(FP8X4), scales=ts[q][:], in_=tg[q][:])
+            w = N // parts
+            for h in range(parts):
+                nc.vector.quantize_mx(
+                    out=tq[q][:, h * w : (h + 1) * w].bitcast(FP8X4),
+                    scales=ts[q][:, h * w : (h + 1) * w],
+                    in_=tg[q][:, 4 * h * w : 4 * (h + 1) * w],
+                )
 
-        def st_g(q):
-            for h in range(2):
-                s2b[q, h] = ps_2.tile([P, 2, NH], F32, name="s2b", tag="s2b")
-                for e in range(2):
-                    rt = 2 * h + e
-                    nc.tensor.matmul_mx(
-                        out=s2b[q, h][:, e, :],
-                        lhsT=tq[q][:, rt * P : (rt + 1) * P].bitcast(FP8X4),
-                        lhsT_scale=ts[q][:, rt * P : (rt + 1) * P],
-                        rhs=h2c[:].bitcast(FP8X4),
-                        rhs_scale=h2s[:],
-                        start=True,
-                        stop=True,
-                    )
+        def p_g(q, h):
+            b = new_bank(("G", q, h))
+            for e in range(2):
+                rt = 2 * h + e
+                nc.tensor.matmul_mx(
+                    out=b[:, e * NH : (e + 1) * NH],
+                    lhsT=tq[q][:, rt * P : (rt + 1) * P].bitcast(FP8X4),
+                    lhsT_scale=ts[q][:, rt * P : (rt + 1) * P],
+                    rhs=h2c[:].bitcast(FP8X4),
+                    rhs_scale=h2s[:],
+                    start=True,
+                    stop=True,
+                )
 
-        def st_h(q):
-            ob[q] = opool.tile([P, 4, NH], F32, name="ob", tag="ob")
-            nc.vector.tensor_copy(out=ob[q][:, 0:2, :], in_=s2b[q, 0][:])
-            nc.scalar.copy(out=ob[q][:, 2:4, :], in_=s2b[q, 1][:])
-
-        def st_i(q):
-            for s in range(4):
+        def e_g(q, h, eng):
+            if q not in ob:
+                ob[q] = opool.tile([P, 4, NH], F32, name="ob", tag="ob")
+            copy_on(eng, ob[q][:, 2 * h : 2 * h + 2, :], bank["G", q, h][:].rearrange("p (e n) -> p e n", e=2))
+            for s in (2 * h, 2 * h + 1):
                 nc.sync.dma_start(out=out_view(q, s), in_=ob[q][:, s, :])
 
-        st_a(0)
-        st_b(0)
-        nc.scalar.copy(out=g2[:], in_=hraw[:, :, 0:NH].rearrange("p j w -> p w j"))
-        nc.vector.tensor_copy(out=g1[:], in_=hraw[:].rearrange("p j (m a) -> p a m j", a=4))
-        st_c(0)
+        def s_quad(q, engs):
+            for rt in range(4):
+                p_s(q, rt)
+            for rt in range(4):
+                e_s(q, rt, engs[rt])
+
+        def g_quad(q, engs):
+            for h in range(2):
+                p_g(q, h)
+            for h in range(2):
+                e_g(q, h, engs[h])
+
+        hperm = hraw[:].rearrange("p j (m a) -> p a m j", a=4)
+
+        for q in (0, 1):
+            p_t(q, 0)
+            p_t(q, 1)
+        e_t(0, 0, V)
+        e_t(0, 1, V)
+        e_t(1, 0, A)
+        c_q(0)
+        nc.vector.tensor_copy(out=g1[:, 0:2, :, :], in_=hperm[:, 0:2, :, :])
+        nc.scalar.copy(out=g1[:, 2:4, :, :], in_=hperm[:, 2:4, :, :])
+        e_t(1, 1, V)
+        nc.vector.tensor_copy(out=g2[:], in_=hraw[:, :, 0:NH].rearrange("p j w -> p w j"))
         nc.vector.quantize_mx(
             out=h1c[:].bitcast(FP8X4), scales=h1s[:], in_=g1[:].rearrange("p a m j -> p (a m j)")
         )
+        c_q(1)
         nc.vector.quantize_mx(
             out=h2c[:].bitcast(FP8X4), scales=h2s[:], in_=g2[:].rearrange("p w j -> p (w j)")
         )
 
-        for i in range(NQ + 1):
-            if i + 1 < NQ:
-                st_a(i + 1)
+        for i in range(7):
+            a, b, c, d = 2 * i, 2 * i + 1, 2 * i + 2, 2 * i + 3
+            for q in (c, d):
+                p_t(q, 0)
+                p_t(q, 1)
             if i >= 1:
-                st_f(i - 1)
-            if i + 1 < NQ:
-                st_b(i + 1)
-            if i < NQ:
-                st_d(i)
-                st_e(i)
-            if i + 1 < NQ:
-                st_c(i + 1)
+                f_q(a - 2, 1)
+                f_q(b - 2, 1)
+            e_t(c, 0, A)
+            e_t(c, 1, A)
+            e_t(d, 0, V)
+            e_t(d, 1, A)
+            c_q(c)
+            c_q(d)
+            s_quad(a, (A, A, V, A))
+            s_quad(b, (V, A, V, A))
             if i >= 1:
-                st_g(i - 1)
-                st_h(i - 1)
-                st_i(i - 1)
+                g_quad(a - 2, (V, A))
+                g_quad(b - 2, (V, A))
+
+        f_q(12, 1)
+        f_q(13, 1)
+        s_quad(14, (A, A, V, A))
+        g_quad(12, (V, A))
+        g_quad(13, (V, A))
+        f_q(14, 2)
+        s_quad(15, (V, A, V, A))
+        f_q(15, 2)
+        g_quad(14, (A, A))
+        g_quad(15, (V, A))

@@ -35,10 +35,10 @@ def tile_mylayer_t_kernel(tc, x, haar, out):
             v = x[b].rearrange("c (l s r) k -> s (c l) r k", l=8, s=2, r=32)
             return v[sg][:, 4 * (q % 4) : 4 * (q % 4) + 4, :]
 
-        def out_view(q, s):
+        def out_view(q, h):
             b, sg = (q // 4) // 2, (q // 4) % 2
-            v = out[b].rearrange("(l s) (i c) n -> s i c l n", s=2, c=16)
-            return v[sg][4 * (q % 4) + s]
+            v = out[b].rearrange("(l g) (j t) n -> g j l (t n)", g=2, t=4)
+            return v[sg][16 * (q % 4) : 16 * (q % 4) + 16, :, 2 * h * NH : (2 * h + 2) * NH]
 
         def copy_on(eng, dst, src):
             if eng == V:
@@ -48,6 +48,11 @@ def tile_mylayer_t_kernel(tc, x, haar, out):
 
         ident = const.tile([P, P], F32, name="ident")
         make_identity(nc, ident[:])
+        perm = const.tile([P, P], F32, name="perm")
+        nc.vector.tensor_copy(
+            out=perm[:].rearrange("p (t h l) -> p t h l", t=4, h=4),
+            in_=ident[:].rearrange("p (h t l) -> p t h l", t=4, h=4),
+        )
 
         xq = {}
         hraw = const.tile([P, 4, N], BF16, name="hraw")
@@ -82,7 +87,7 @@ def tile_mylayer_t_kernel(tc, x, haar, out):
             b = new_bank(("T", q, h))[:].rearrange("p (u r) -> p u r", u=2)
             for e in range(2):
                 for u in range(2):
-                    nc.tensor.transpose(b[:, u, e * P : (e + 1) * P], xw[:, 2 * h + e, u:256:2], ident[:])
+                    nc.tensor.transpose(b[:, u, e * P : (e + 1) * P], xw[:, 2 * h + e, u:256:2], perm[:])
 
         def e_t(q, h, eng):
             if q not in rg:
@@ -113,8 +118,8 @@ def tile_mylayer_t_kernel(tc, x, haar, out):
                 tg[q] = work.tile([P, 4 * N], BF16, name="tg", tag="tg", align_bytes=64)
             copy_on(
                 eng,
-                tg[q][:, rt * N : (rt + 1) * N].rearrange("p (r a) -> p r a", a=4),
-                bank["S", q, rt][:].rearrange("p (a r) -> p r a", a=4),
+                tg[q][:].rearrange("p (t s i a) -> p s t i a", t=4, s=4, a=4)[:, rt],
+                bank["S", q, rt][:].rearrange("p (a t i) -> p t i a", a=4, t=4),
             )
 
         def f_q(q, parts):
@@ -146,8 +151,7 @@ def tile_mylayer_t_kernel(tc, x, haar, out):
             if q not in ob:
                 ob[q] = opool.tile([P, 4, NH], F32, name="ob", tag="ob")
             copy_on(eng, ob[q][:, 2 * h : 2 * h + 2, :], bank["G", q, h][:].rearrange("p (e n) -> p e n", e=2))
-            for s in (2 * h, 2 * h + 1):
-                nc.sync.dma_start(out=out_view(q, s), in_=ob[q][:, s, :])
+            nc.sync.dma_start(out=out_view(q, h), in_=ob[q][:, 2 * h : 2 * h + 2, :].rearrange("p t n -> p (t n)"))
 
         def s_quad(q, engs):
             for rt in range(4):

@@ -35,10 +35,10 @@ def tile_mylayer_t_kernel(tc, x, haar, out):
             v = x[b].rearrange("c (l s r) k -> s (c l) r k", l=8, s=2, r=32)
             return v[sg][:, 4 * (q % 4) : 4 * (q % 4) + 4, :]
 
-        def out_view(q, h):
+        def out_view(q, s):
             b, sg = (q // 4) // 2, (q // 4) % 2
-            v = out[b].rearrange("(l g) (j t) n -> g j l (t n)", g=2, t=4)
-            return v[sg][16 * (q % 4) : 16 * (q % 4) + 16, :, 2 * h * NH : (2 * h + 2) * NH]
+            v = out[b].rearrange("(l s) (i c) n -> s i c l n", s=2, c=16)
+            return v[sg][4 * (q % 4) + s]
 
         def copy_on(eng, dst, src):
             if eng == V:
@@ -48,11 +48,6 @@ def tile_mylayer_t_kernel(tc, x, haar, out):
 
         ident = const.tile([P, P], F32, name="ident")
         make_identity(nc, ident[:])
-        perm = const.tile([P, P], F32, name="perm")
-        nc.vector.tensor_copy(
-            out=perm[:].rearrange("p (t h l) -> p t h l", t=4, h=4),
-            in_=ident[:].rearrange("p (h t l) -> p t h l", t=4, h=4),
-        )
 
         xq = {}
         hraw = const.tile([P, 4, N], BF16, name="hraw")
@@ -63,7 +58,7 @@ def tile_mylayer_t_kernel(tc, x, haar, out):
                 nc.sync.dma_start(out=xq[0][:, 2:4, :], in_=x_view(0)[:, 2:4, :])
             else:
                 nc.sync.dma_start(out=xq[q][:], in_=x_view(q))
-            if q == 1:
+            if q == 0:
                 nc.sync.dma_start(out=hraw[:], in_=haar.rearrange("(p j) w -> p j w", j=4))
 
         g1 = const.tile([P, 4, P, 4], BF16, name="g1", align_bytes=64)
@@ -87,7 +82,7 @@ def tile_mylayer_t_kernel(tc, x, haar, out):
             b = new_bank(("T", q, h))[:].rearrange("p (u r) -> p u r", u=2)
             for e in range(2):
                 for u in range(2):
-                    nc.tensor.transpose(b[:, u, e * P : (e + 1) * P], xw[:, 2 * h + e, u:256:2], perm[:])
+                    nc.tensor.transpose(b[:, u, e * P : (e + 1) * P], xw[:, 2 * h + e, u:256:2], ident[:])
 
         def e_t(q, h, eng):
             if q not in rg:
@@ -118,8 +113,8 @@ def tile_mylayer_t_kernel(tc, x, haar, out):
                 tg[q] = work.tile([P, 4 * N], BF16, name="tg", tag="tg", align_bytes=64)
             copy_on(
                 eng,
-                tg[q][:].rearrange("p (t s i a) -> p s t i a", t=4, s=4, a=4)[:, rt],
-                bank["S", q, rt][:].rearrange("p (a t i) -> p t i a", a=4, t=4),
+                tg[q][:, rt * N : (rt + 1) * N].rearrange("p (r a) -> p r a", a=4),
+                bank["S", q, rt][:].rearrange("p (a r) -> p r a", a=4),
             )
 
         def f_q(q, parts):
@@ -151,7 +146,8 @@ def tile_mylayer_t_kernel(tc, x, haar, out):
             if q not in ob:
                 ob[q] = opool.tile([P, 4, NH], F32, name="ob", tag="ob")
             copy_on(eng, ob[q][:, 2 * h : 2 * h + 2, :], bank["G", q, h][:].rearrange("p (e n) -> p e n", e=2))
-            nc.sync.dma_start(out=out_view(q, h), in_=ob[q][:, 2 * h : 2 * h + 2, :].rearrange("p t n -> p (t n)"))
+            for s in (2 * h, 2 * h + 1):
+                nc.sync.dma_start(out=out_view(q, s), in_=ob[q][:, s, :])
 
         def s_quad(q, engs):
             for rt in range(4):
@@ -167,33 +163,46 @@ def tile_mylayer_t_kernel(tc, x, haar, out):
 
         hperm = hraw[:].rearrange("p j (m a) -> p a m j", a=4)
 
-        for q in (0, 1):
-            p_t(q, 0)
-            p_t(q, 1)
+        p_t(0, 0)
+        p_t(0, 1)
         e_t(0, 0, V)
-        e_t(0, 1, V)
-        e_t(1, 0, A)
-        c_q(0)
+        e_t(0, 1, A)
         nc.vector.tensor_copy(out=g1[:, 0:2, :, :], in_=hperm[:, 0:2, :, :])
         nc.scalar.copy(out=g1[:, 2:4, :, :], in_=hperm[:, 2:4, :, :])
-        e_t(1, 1, V)
-        nc.vector.tensor_copy(out=g2[:], in_=hraw[:, :, 0:NH].rearrange("p j w -> p w j"))
+        c_q(0)
         nc.vector.quantize_mx(
             out=h1c[:].bitcast(FP8X4), scales=h1s[:], in_=g1[:].rearrange("p a m j -> p (a m j)")
         )
+        p_t(1, 0)
+        p_t(1, 1)
+        e_t(1, 0, A)
+        e_t(1, 1, V)
+        s_quad(0, (A, V, A, V))
         c_q(1)
+        nc.vector.tensor_copy(out=g2[:], in_=hraw[:, :, 0:NH].rearrange("p j w -> p w j"))
         nc.vector.quantize_mx(
             out=h2c[:].bitcast(FP8X4), scales=h2s[:], in_=g2[:].rearrange("p w j -> p (w j)")
         )
+        for q in (2, 3):
+            p_t(q, 0)
+            p_t(q, 1)
+        e_t(2, 0, A)
+        e_t(2, 1, A)
+        e_t(3, 0, V)
+        e_t(3, 1, A)
+        c_q(2)
+        c_q(3)
+        s_quad(1, (A, V, A, V))
+        f_q(0, 1)
 
-        for i in range(7):
+        for i in range(1, 7):
             a, b, c, d = 2 * i, 2 * i + 1, 2 * i + 2, 2 * i + 3
             for q in (c, d):
                 p_t(q, 0)
                 p_t(q, 1)
-            if i >= 1:
+            if i >= 2:
                 f_q(a - 2, 1)
-                f_q(b - 2, 1)
+            f_q(b - 2, 1)
             e_t(c, 0, A)
             e_t(c, 1, A)
             e_t(d, 0, V)
@@ -202,9 +211,8 @@ def tile_mylayer_t_kernel(tc, x, haar, out):
             c_q(d)
             s_quad(a, (A, A, V, A))
             s_quad(b, (V, A, V, A))
-            if i >= 1:
-                g_quad(a - 2, (V, A))
-                g_quad(b - 2, (V, A))
+            g_quad(a - 2, (V, A))
+            g_quad(b - 2, (V, A))
 
         f_q(12, 1)
         f_q(13, 1)

@@ -58,7 +58,7 @@ def tile_mylayer_t_kernel(tc, x, haar, out):
                 nc.sync.dma_start(out=xq[0][:, 2:4, :], in_=x_view(0)[:, 2:4, :])
             else:
                 nc.sync.dma_start(out=xq[q][:], in_=x_view(q))
-            if q == 0:
+            if q == 1:
                 nc.sync.dma_start(out=hraw[:], in_=haar.rearrange("(p j) w -> p j w", j=4))
 
         g1 = const.tile([P, 4, P, 4], BF16, name="g1", align_bytes=64)
@@ -163,56 +163,44 @@ def tile_mylayer_t_kernel(tc, x, haar, out):
 
         hperm = hraw[:].rearrange("p j (m a) -> p a m j", a=4)
 
-        p_t(0, 0)
-        p_t(0, 1)
+        for q in (0, 1):
+            p_t(q, 0)
+            p_t(q, 1)
         e_t(0, 0, V)
         e_t(0, 1, A)
+        e_t(1, 0, A)
+        c_q(0)
         nc.vector.tensor_copy(out=g1[:, 0:2, :, :], in_=hperm[:, 0:2, :, :])
         nc.scalar.copy(out=g1[:, 2:4, :, :], in_=hperm[:, 2:4, :, :])
-        c_q(0)
+        e_t(1, 1, V)
+        nc.vector.tensor_copy(out=g2[:], in_=hraw[:, :, 0:NH].rearrange("p j w -> p w j"))
         nc.vector.quantize_mx(
             out=h1c[:].bitcast(FP8X4), scales=h1s[:], in_=g1[:].rearrange("p a m j -> p (a m j)")
         )
-        p_t(1, 0)
-        p_t(1, 1)
-        e_t(1, 0, A)
-        e_t(1, 1, V)
-        s_quad(0, (A, V, A, V))
         c_q(1)
-        nc.vector.tensor_copy(out=g2[:], in_=hraw[:, :, 0:NH].rearrange("p j w -> p w j"))
         nc.vector.quantize_mx(
             out=h2c[:].bitcast(FP8X4), scales=h2s[:], in_=g2[:].rearrange("p w j -> p (w j)")
         )
-        for q in (2, 3):
-            p_t(q, 0)
-            p_t(q, 1)
-        e_t(2, 0, A)
-        e_t(2, 1, A)
-        e_t(3, 0, V)
-        e_t(3, 1, A)
-        c_q(2)
-        c_q(3)
-        s_quad(1, (A, V, A, V))
-        f_q(0, 1)
 
-        for i in range(1, 7):
+        for i in range(7):
             a, b, c, d = 2 * i, 2 * i + 1, 2 * i + 2, 2 * i + 3
             for q in (c, d):
                 p_t(q, 0)
                 p_t(q, 1)
-            if i >= 2:
+            if i >= 1:
                 f_q(a - 2, 1)
-            f_q(b - 2, 1)
+                f_q(b - 2, 1)
             e_t(c, 0, A)
             e_t(c, 1, A)
-            e_t(d, 0, V)
+            e_t(d, 0, A if i % 2 == 1 else V)
             e_t(d, 1, A)
             c_q(c)
             c_q(d)
             s_quad(a, (A, A, V, A))
             s_quad(b, (V, A, V, A))
-            g_quad(a - 2, (V, A))
-            g_quad(b - 2, (V, A))
+            if i >= 1:
+                g_quad(a - 2, (V, A))
+                g_quad(b - 2, (V, A))
 
         f_q(12, 1)
         f_q(13, 1)

from contextlib import ExitStack

import concourse.mybir as mybir
from concourse.masks import make_identity

F32 = mybir.dt.float32
BF16 = mybir.dt.bfloat16
U32 = mybir.dt.uint32
U8 = mybir.dt.uint8
FP8X4 = mybir.dt.float8_e4m3fn_x4

P = 128
N = 512
NH = 256
ROWS = 8192
FLOPS = 2 * ROWS * N * N + 2 * ROWS * N * NH
BYTES = ROWS * N * 2 + N * N * 2 + ROWS * NH * 4
NQ = 16
V = "vector"
A = "scalar"


def tile_mylayer_t_kernel(tc, x, haar, out):
    nc = tc.nc
    with ExitStack() as ctx:
        const = ctx.enter_context(tc.tile_pool(name="const", bufs=1))
        xpool = ctx.enter_context(tc.tile_pool(name="xpool", bufs=NQ))
        work = ctx.enter_context(tc.tile_pool(name="work", bufs=4))
        opool = ctx.enter_context(tc.tile_pool(name="opool", bufs=6))
        psum = ctx.enter_context(tc.psum_pool(name="psum", bufs=1))
        ctx.enter_context(tc.manual_schedule())

        def x_view(q):
            b, sg = (q // 4) // 2, (q // 4) % 2
            v = x[b].rearrange("c (l s r) k -> s (c l) r k", l=8, s=2, r=32)
            return v[sg][:, 4 * (q % 4) : 4 * (q % 4) + 4, :]

        def out_view(q, s):
            b, sg = (q // 4) // 2, (q // 4) % 2
            v = out[b].rearrange("(l s) (i c) n -> s i c l n", s=2, c=16)
            return v[sg][4 * (q % 4) + s]

        def copy_on(eng, dst, src):
            if eng == V:
                nc.vector.tensor_copy(out=dst, in_=src)
            else:
                nc.scalar.copy(out=dst, in_=src)

        ident = const.tile([P, P], F32, name="ident")
        make_identity(nc, ident[:])

        xq = {}
        hraw = const.tile([P, 4, N], BF16, name="hraw")
        for q in range(NQ):
            xq[q] = xpool.tile([P, 4, N], BF16, name="xq", tag="xq")
            if q == 0:
                nc.sync.dma_start(out=xq[0][:, 0:2, :], in_=x_view(0)[:, 0:2, :])
                nc.sync.dma_start(out=xq[0][:, 2:4, :], in_=x_view(0)[:, 2:4, :])
            else:
                nc.sync.dma_start(out=xq[q][:], in_=x_view(q))
            if q == 1:
                nc.sync.dma_start(out=hraw[:], in_=haar.rearrange("(p j) w -> p j w", j=4))

        g1 = const.tile([P, 4, P, 4], BF16, name="g1", align_bytes=64)
        g2 = const.tile([P, NH, 4], BF16, name="g2", align_bytes=64)
        h1c = const.tile([P, N], U32, name="h1c", align_bytes=64)
        h1s = const.tile([P, N], U8, name="h1s", align_bytes=64)
        h2c = const.tile([P, NH], U32, name="h2c", align_bytes=64)
        h2s = const.tile([P, NH], U8, name="h2s", align_bytes=64)

        ring = [0]
        bank, rg, rc, rs, tg, tq, ts, ob = {}, {}, {}, {}, {}, {}, {}, {}

        def new_bank(key):
            k = ring[0] % 8
            ring[0] = ring[0] + 1
            bank[key] = psum.tile([P, N], F32, name="bank%d" % k, tag="bank%d" % k)
            return bank[key]

        def p_t(q, h):
            xw = xq[q][:].bitcast(F32)
            b = new_bank(("T", q, h))[:].rearrange("p (u r) -> p u r", u=2)
            for e in range(2):
                for u in range(2):
                    nc.tensor.transpose(b[:, u, e * P : (e + 1) * P], xw[:, 2 * h + e, u:256:2], ident[:])

        def e_t(q, h, eng):
            if q not in rg:
                rg[q] = work.tile([P, 4 * N], BF16, name="rg", tag="rg", align_bytes=64)
            rw = rg[q][:].bitcast(F32).rearrange("p (r u) -> p r u", u=2)
            copy_on(eng, rw[:, h * 256 : (h + 1) * 256, :], bank["T", q, h][:].rearrange("p (u r) -> p r u", u=2))

        def c_q(q):
            rc[q] = work.tile([P, N], U32, name="rc", tag="rc", align_bytes=64)
            rs[q] = work.tile([P, N], U8, name="rs", tag="rs", align_bytes=64)
            nc.vector.quantize_mx(out=rc[q][:].bitcast(FP8X4), scales=rs[q][:], in_=rg[q][:])

        def p_s(q, rt):
            b = new_bank(("S", q, rt))
            for a in range(4):
                nc.tensor.matmul_mx(
                    out=b[:, a * P : (a + 1) * P],
                    lhsT=h1c[:, a * P : (a + 1) * P].bitcast(FP8X4),
                    lhsT_scale=h1s[:, a * P : (a + 1) * P],
                    rhs=rc[q][:, rt * P : (rt + 1) * P].bitcast(FP8X4),
                    rhs_scale=rs[q][:, rt * P : (rt + 1) * P],
                    start=True,
                    stop=True,
                )

        def e_s(q, rt, eng):
            if q not in tg:
                tg[q] = work.tile([P, 4 * N], BF16, name="tg", tag="tg", align_bytes=64)
            copy_on(
                eng,
                tg[q][:, rt * N : (rt + 1) * N].rearrange("p (r a) -> p r a", a=4),
                bank["S", q, rt][:].rearrange("p (a r) -> p r a", a=4),
            )

        def f_q(q, parts):
            tq[q] = work.tile([P, N], U32, name="tq", tag="tq", align_bytes=64)
            ts[q] = work.tile([P, N], U8, name="ts", tag="ts", align_bytes=64)
            w = N // parts
            for h in range(parts):
                nc.vector.quantize_mx(
                    out=tq[q][:, h * w : (h + 1) * w].bitcast(FP8X4),
                    scales=ts[q][:, h * w : (h + 1) * w],
                    in_=tg[q][:, 4 * h * w : 4 * (h + 1) * w],
                )

        def p_g(q, h):
            b = new_bank(("G", q, h))
            for e in range(2):
                rt = 2 * h + e
                nc.tensor.matmul_mx(
                    out=b[:, e * NH : (e + 1) * NH],
                    lhsT=tq[q][:, rt * P : (rt + 1) * P].bitcast(FP8X4),
                    lhsT_scale=ts[q][:, rt * P : (rt + 1) * P],
                    rhs=h2c[:].bitcast(FP8X4),
                    rhs_scale=h2s[:],
                    start=True,
                    stop=True,
                )

        def e_g(q, h, eng):
            if q not in ob:
                ob[q] = opool.tile([P, 4, NH], F32, name="ob", tag="ob")
            copy_on(eng, ob[q][:, 2 * h : 2 * h + 2, :], bank["G", q, h][:].rearrange("p (e n) -> p e n", e=2))
            for s in (2 * h, 2 * h + 1):
                nc.sync.dma_start(out=out_view(q, s), in_=ob[q][:, s, :])

        def s_quad(q, engs):
            for rt in range(4):
                p_s(q, rt)
            for rt in range(4):
                e_s(q, rt, engs[rt])

        def g_quad(q, engs):
            for h in range(2):
                p_g(q, h)
            for h in range(2):
                e_g(q, h, engs[h])

        hperm = hraw[:].rearrange("p j (m a) -> p a m j", a=4)

        for q in (0, 1):
            p_t(q, 0)
            p_t(q, 1)
        e_t(0, 0, V)
        e_t(0, 1, A)
        e_t(1, 0, A)
        c_q(0)
        nc.vector.tensor_copy(out=g1[:, 0:2, :, :], in_=hperm[:, 0:2, :, :])
        nc.scalar.copy(out=g1[:, 2:4, :, :], in_=hperm[:, 2:4, :, :])
        e_t(1, 1, V)
        nc.vector.tensor_copy(out=g2[:], in_=hraw[:, :, 0:NH].rearrange("p j w -> p w j"))
        nc.vector.quantize_mx(
            out=h1c[:].bitcast(FP8X4), scales=h1s[:], in_=g1[:].rearrange("p a m j -> p (a m j)")
        )
        c_q(1)
        nc.vector.quantize_mx(
            out=h2c[:].bitcast(FP8X4), scales=h2s[:], in_=g2[:].rearrange("p w j -> p (w j)")
        )

        for i in range(7):
            a, b, c, d = 2 * i, 2 * i + 1, 2 * i + 2, 2 * i + 3
            for q in (c, d):
                p_t(q, 0)
                p_t(q, 1)
            if i >= 1:
                f_q(a - 2, 1)
                f_q(b - 2, 1)
            e_t(c, 0, A)
            e_t(c, 1, A)
            e_t(d, 0, A if i % 2 == 1 else V)
            e_t(d, 1, A)
            c_q(c)
            c_q(d)
            s_quad(a, (A, A, V, A))
            s_quad(b, (V, A, V, A))
            if i >= 1:
                g_quad(a - 2, (V, A))
                g_quad(b - 2, (V, A))

        f_q(12, 1)
        f_q(13, 1)
        s_quad(14, (A, A, V, A))
        g_quad(12, (V, A))
        g_quad(13, (V, A))
        f_q(14, 2)
        s_quad(15, (V, A, V, A))
        f_q(15, 2)
        g_quad(14, (A, A))
        g_quad(15, (V, A))
